import numpy as np
import ml_dtypes


def mxq(x, axis, fmt="e4m3"):
    dtype, down = {"e4m3": (ml_dtypes.float8_e4m3fn, 7), "e5m2": (ml_dtypes.float8_e5m2, 14)}[fmt]
    v = np.moveaxis(np.asarray(x, np.float32).astype(ml_dtypes.bfloat16).astype(np.float64), axis, -1)
    blocks = v.reshape(v.shape[:-1] + (-1, 32))
    amax = np.abs(blocks).max(-1, keepdims=True)
    byte = np.maximum(np.where(amax > 0, np.frexp(amax)[1] - 1 + 127, 0) - down, 1)
    scale = np.exp2(byte - 127.0)
    codes = (blocks / scale).astype(np.float32).astype(dtype).astype(np.float64)
    return np.moveaxis((codes * scale).reshape(v.shape), -1, axis)


WIDE = False


def mx_kscale(k):
    if not WIDE:
        return np.ones(k)
    levels = np.array([10, -10, 5, -5, 0])
    a = np.random.permutation(np.resize(levels, k // 512 * 4)).reshape(k // 512, 4)
    idx = np.arange(k)
    return np.exp2(a[idx // 512, idx % 128 // 32])


BF16 = ml_dtypes.bfloat16


def bf(x):
    return np.asarray(x, np.float32).astype(BF16)


def f64(x):
    return np.asarray(x).astype(np.float64)


E2M1 = np.array([0.0, 0.5, 1.0, 1.5, 2.0, 3.0, 4.0, 6.0, -0.0, -0.5, -1.0, -1.5, -2.0, -3.0, -4.0, -6.0])


def pack_weight(w, fmt):
    k, n = w.shape
    w = f64(bf(w)).reshape(k // 32, 32, n)
    amax = np.abs(w).max(1)
    if fmt == "e4m3":
        byte = np.frexp(amax)[1] - 1 + 127 - 7
    else:
        mant, ex = np.frexp(amax / 6.0)
        byte = np.where(mant > 0.5, ex, ex - 1) + 127
    byte = np.clip(np.where(amax > 0, byte, 1), 1, 254)
    scaled = (w * np.exp2(127.0 - byte)[:, None, :]).reshape(k, n).astype(np.float32)
    by_word = np.ascontiguousarray(scaled.reshape(k // 512, 128, 4, n).transpose(0, 1, 3, 2))
    if fmt == "e4m3":
        words = by_word.astype(ml_dtypes.float8_e4m3fn).view(np.uint8)
    else:
        c = by_word.astype(ml_dtypes.float4_e2m1fn).view(np.uint8) & 0xF
        words = c[..., 0::2] | (c[..., 1::2] << 4)
    return np.ascontiguousarray(words), np.ascontiguousarray(byte.astype(np.uint8).reshape(k // 512, 16, n))


def unpack_weight(words, scales, fmt):
    g, p, n, _ = words.shape
    if fmt == "e4m3":
        vals = np.ascontiguousarray(words).view(ml_dtypes.float8_e4m3fn).astype(np.float64)
    else:
        nib = np.empty((g, p, n, 4), np.uint8)
        nib[..., 0::2] = words & 0xF
        nib[..., 1::2] = words >> 4
        vals = E2M1[nib]
    vals = vals * np.repeat(np.exp2(scales.astype(np.float64) - 127.0), 8, axis=1)[..., None]
    return vals.transpose(0, 1, 3, 2).reshape(g * 512, n)


B, N, D, H, DH, WS = 1, 1024, 8192, 8, 32, 512
INNER = H * DH
NW = N // WS
BW = B * NW
FMT = "e4m3"


def elu(u):
    return np.where(u > 0.0, u, np.exp(np.minimum(u, 0.0)) - 1.0)


def heads(t):
    return t.reshape(BW, WS, H, DH).transpose(0, 2, 1, 3)


def setup_inputs():
    s = mx_kscale(D)
    x = bf(np.random.standard_normal((B, N, D)) * s)
    k_words, k_scales = pack_weight(np.random.standard_normal((D, INNER)) / np.sqrt(D) / s[:, None], FMT)
    v_words, v_scales = pack_weight(np.random.standard_normal((D, INNER)) * 0.3 / np.sqrt(D * WS) / s[:, None], FMT)
    return {"x": x,
            "w_k_words": k_words, "w_k_scales": k_scales,
            "w_v_words": v_words, "w_v_scales": v_scales}


def reference(x, w_k_words, w_k_scales, w_v_words, w_v_scales):
    xq = mxq(f64(x).reshape(BW, WS, D), 2, "e4m3")
    k = heads(xq @ unpack_weight(w_k_words, w_k_scales, FMT))
    v = heads(xq @ unpack_weight(w_v_words, w_v_scales, FMT))
    kf = elu(k) + 1.0
    return mxq(kf, 2, "e4m3").transpose(0, 1, 3, 2) @ mxq(v, 2, "e4m3")

@@ -1,0 +1,285 @@
+from contextlib import ExitStack
+
+import concourse.mybir as mybir
+from concourse.masks import make_identity
+
+F32 = mybir.dt.float32
+BF16 = mybir.dt.bfloat16
+I32 = mybir.dt.int32
+U32 = mybir.dt.uint32
+U8 = mybir.dt.uint8
+FP8X4 = mybir.dt.float8_e4m3fn_x4
+ACT = mybir.ActivationFunctionType
+ALU = mybir.AluOpType
+
+P = 128
+PACK = 4
+K_PASS = P * PACK
+
+TOKENS = 1024
+FEATURES = 8192
+WINDOW = 512
+WINDOWS = TOKENS // WINDOW
+HEADS = 8
+HEAD_DIM = 32
+INNER = HEADS * HEAD_DIM
+COLS = 2 * INNER
+
+GROUPS = FEATURES // K_PASS
+WINDOW_TILES = WINDOW // P
+TOKEN_TILES = TOKENS // P
+CHUNK_GROUPS = 4
+CHUNKS = GROUPS // CHUNK_GROUPS
+BLOCK_FEATURES = CHUNK_GROUPS * K_PASS
+BLOCK_PAIRS = BLOCK_FEATURES // 2
+BANK_GROUPS = 2
+LOAD_GROUPS = 2
+RUN_BLOCKS = 2
+QUADRANT = 32
+HALF_HEADS = P // HEAD_DIM
+
+FLOPS = 2 * TOKENS * FEATURES * COLS + 2 * WINDOWS * HEADS * WINDOW * HEAD_DIM * HEAD_DIM
+
+
+def tile_localcontextprocessor_pa_k_kernel(
+    tc, x, w_k_words, w_k_scales, w_v_words, w_v_scales, out
+):
+    nc = tc.nc
+
+    blocks = [(t, c) for c in range(CHUNKS) for t in range(WINDOW_TILES)]
+    blocks += [(t, c) for t in range(WINDOW_TILES, TOKEN_TILES) for c in range(CHUNKS)]
+    runs = [blocks[i : i + RUN_BLOCKS] for i in range(0, len(blocks), RUN_BLOCKS)]
+
+    x_tiles = x.flatten_outer_dims().rearrange("(w p j) d -> w j p d", p=P, j=PACK)
+    out_rows = out.rearrange("w (a h) d e -> (h d) w a e", a=HEADS // HALF_HEADS)
+    weight_words = [(w_k_words, 0), (w_v_words, INNER)]
+    weight_scales = [(w_k_scales, 0), (w_v_scales, INNER)]
+
+    with ExitStack() as stack:
+        consts = stack.enter_context(tc.tile_pool(name="consts", bufs=1))
+        weights = stack.enter_context(tc.tile_pool(name="weights", bufs=1))
+        x_pool = stack.enter_context(tc.tile_pool(name="x_pool", bufs=len(blocks)))
+        stream = stack.enter_context(tc.tile_pool(name="stream", bufs=2 * RUN_BLOCKS))
+        per_tile = stack.enter_context(tc.tile_pool(name="per_tile", bufs=2))
+        window_pool = stack.enter_context(tc.tile_pool(name="window_pool", bufs=1))
+        flip_psum = stack.enter_context(tc.psum_pool(name="flip_psum", bufs=4))
+        acc_psum = stack.enter_context(tc.psum_pool(name="acc_psum", bufs=4))
+        stack.enter_context(tc.manual_schedule())
+
+        warm = consts.tile([P, 1], F32)
+        nc.vector.memset(warm[:], 0.0)
+        nc.scalar.activation(out=warm[:], in_=warm[:], func=ACT.Exp)
+        identity = consts.tile([P, P], F32)
+        make_identity(nc, identity[:])
+
+        x_raw_of = {}
+
+        def load_x(t, c):
+            x_raw = x_pool.tile([P, BLOCK_FEATURES], BF16)
+            nc.sync.dma_start(
+                out=x_raw[:],
+                in_=x_tiles[
+                    t // WINDOW_TILES,
+                    t % WINDOW_TILES,
+                    :,
+                    c * BLOCK_FEATURES : (c + 1) * BLOCK_FEATURES,
+                ],
+            )
+            x_raw_of[(t, c)] = x_raw
+
+        w_planes = weights.tile([P, GROUPS, COLS], U8, align_bytes=64)
+        nc.vector.memset(w_planes[:].rearrange("p g n -> p (g n)").bitcast(I32), 0)
+
+        def load_weight_planes():
+            for scales, first_col in weight_scales:
+                rows = scales.bitcast(I32).rearrange("g (q r) n -> r q g n", r=PACK)
+                for r in range(PACK):
+                    nc.sync.dma_start(
+                        out=w_planes[
+                            r:P:QUADRANT, :, first_col : first_col + INNER
+                        ].bitcast(I32),
+                        in_=rows[r],
+                    )
+
+        w_words_of = {}
+
+        def load_weight_words(first_group):
+            w_words = weights.tile(
+                [P, LOAD_GROUPS, COLS], U32, name="w_words_%d" % first_group, align_bytes=64
+            )
+            for words, first_col in weight_words:
+                rows = (
+                    words.rearrange("g p n t -> g p (n t)")
+                    .bitcast(I32)
+                    .rearrange("g p n -> p g n")
+                )
+                nc.sync.dma_start(
+                    out=w_words[:, :, first_col : first_col + INNER].bitcast(I32),
+                    in_=rows[:, first_group : first_group + LOAD_GROUPS, :],
+                )
+            for g in range(LOAD_GROUPS):
+                w_words_of[first_group + g] = w_words[:, g, :]
+
+        for c in range(CHUNKS):
+            for t in range(WINDOW_TILES):
+                load_x(t, c)
+            if c == 0:
+                load_weight_planes()
+            for g in range(c * CHUNK_GROUPS, (c + 1) * CHUNK_GROUPS, LOAD_GROUPS):
+                load_weight_words(g)
+        for t, c in blocks[CHUNKS * WINDOW_TILES :]:
+            load_x(t, c)
+
+        x_sorted_of = {}
+        grouped_of = {}
+        x_codes_of = {}
+        acc_of = {}
+
+        def sort_pairs(block):
+            x_sorted = stream.tile([P, CHUNK_GROUPS, 2, P], F32)
+            nc.vector.tensor_copy(
+                out=x_sorted[:],
+                in_=x_raw_of[block][:]
+                .bitcast(F32)
+                .rearrange("p (g i u) -> p g u i", g=CHUNK_GROUPS, u=2),
+            )
+            x_sorted_of[block] = x_sorted
+
+        def transpose_and_copy_out(block):
+            x_sorted = x_sorted_of[block]
+            grouped = stream.tile([P, BLOCK_FEATURES], BF16, align_bytes=64)
+            grouped_pairs = (
+                grouped[:].bitcast(F32).rearrange("p (g t u) -> p g t u", g=CHUNK_GROUPS, u=2)
+            )
+            for g0 in range(0, CHUNK_GROUPS, BANK_GROUPS):
+                flipped = flip_psum.tile([P, BANK_GROUPS, 2, P], F32)
+                for g in range(BANK_GROUPS):
+                    for u in range(2):
+                        nc.tensor.transpose(
+                            flipped[:, g, u, :], x_sorted[:, g0 + g, u, :], identity[:]
+                        )
+                nc.scalar.copy(
+                    out=grouped_pairs[:, g0 : g0 + BANK_GROUPS],
+                    in_=flipped[:].rearrange("p g u t -> p g t u"),
+                )
+            grouped_of[block] = grouped
+
+        def quantise_x(block):
+            x_words = stream.tile([P, CHUNK_GROUPS * P], U32, align_bytes=64)
+            x_plane = stream.tile([P, CHUNK_GROUPS * P], U8, align_bytes=64)
+            nc.vector.quantize_mx(
+                out=x_words[:].bitcast(FP8X4), scales=x_plane[:], in_=grouped_of[block][:]
+            )
+            x_codes_of[block] = (x_words, x_plane)
+
+        def project(block):
+            t, c = block
+            if c == 0:
+                acc = acc_psum.tile([P, COLS], F32)
+                acc_of[t] = acc
+            x_words, x_plane = x_codes_of[block]
+            for g in range(CHUNK_GROUPS):
+                group = c * CHUNK_GROUPS + g
+                tokens = slice(g * P, (g + 1) * P)
+                nc.tensor.matmul_mx(
+                    out=acc_of[t][:],
+                    lhsT=x_words[:, tokens].bitcast(FP8X4),
+                    lhsT_scale=x_plane[:, tokens],
+                    rhs=w_words_of[group].bitcast(FP8X4),
+                    rhs_scale=w_planes[:, group, :],
+                    start=(group == 0),
+                    stop=(group == GROUPS - 1),
+                )
+
+        window_tiles_of = {}
+
+        def finish_token_tile(t):
+            w, j = t // WINDOW_TILES, t % WINDOW_TILES
+            if j == 0:
+                kf_grouped = window_pool.tile([P, INNER, PACK], BF16, align_bytes=64)
+                v_grouped = window_pool.tile([P, INNER, PACK], BF16, align_bytes=64)
+                window_tiles_of[w] = (kf_grouped, v_grouped)
+            kf_grouped, v_grouped = window_tiles_of[w]
+            acc = acc_of[t]
+            exp_k = per_tile.tile([P, INNER], F32)
+            relu_k = per_tile.tile([P, INNER], F32)
+            nc.scalar.activation(out=exp_k[:], in_=acc[:, 0:INNER], func=ACT.Exp)
+            nc.scalar.activation(out=relu_k[:], in_=acc[:, 0:INNER], func=ACT.Relu)
+            nc.vector.scalar_tensor_tensor(
+                out=kf_grouped[:, :, j],
+                in0=exp_k[:],
+                scalar=1.0,
+                in1=relu_k[:],
+                op0=ALU.min,
+                op1=ALU.add,
+            )
+            nc.scalar.copy(out=v_grouped[:, :, j], in_=acc[:, INNER:COLS])
+
+        window_codes_of = {}
+
+        def quantise_window(w):
+            kf_grouped, v_grouped = window_tiles_of[w]
+            kf_words = window_pool.tile([P, INNER], U32, align_bytes=64)
+            kf_plane = window_pool.tile([P, INNER], U8, align_bytes=64)
+            v_words = window_pool.tile([P, INNER], U32, align_bytes=64)
+            v_plane = window_pool.tile([P, INNER], U8, align_bytes=64)
+            nc.vector.quantize_mx(
+                out=kf_words[:].bitcast(FP8X4),
+                scales=kf_plane[:],
+                in_=kf_grouped[:].rearrange("p n j -> p (n j)"),
+            )
+            nc.vector.quantize_mx(
+                out=v_words[:].bitcast(FP8X4),
+                scales=v_plane[:],
+                in_=v_grouped[:].rearrange("p n j -> p (n j)"),
+            )
+            window_codes_of[w] = (kf_words, kf_plane, v_words, v_plane)
+
+        def window_context(w):
+            kf_words, kf_plane, v_words, v_plane = window_codes_of[w]
+            products = acc_psum.tile([P, HEADS // HALF_HEADS, P], F32, tag="acc")
+            for a in range(HEADS // HALF_HEADS):
+                cols = slice(a * P, (a + 1) * P)
+                nc.tensor.matmul_mx(
+                    out=products[:, a, :],
+                    lhsT=kf_words[:, cols].bitcast(FP8X4),
+                    lhsT_scale=kf_plane[:, cols],
+                    rhs=v_words[:, cols].bitcast(FP8X4),
+                    rhs_scale=v_plane[:, cols],
+                    start=True,
+                    stop=True,
+                )
+            context = window_pool.tile([P, HEADS // HALF_HEADS, HEAD_DIM], F32)
+            for h in range(HALF_HEADS):
+                rows = slice(h * HEAD_DIM, (h + 1) * HEAD_DIM)
+                nc.vector.tensor_copy(out=context[rows], in_=products[rows, :, rows])
+            nc.sync.dma_start(out=out_rows[:, w], in_=context[:])
+
+        closed_tiles = []
+        tiles_finished = 0
+        windows_quantised = 0
+        windows_done = 0
+        for s in range(len(runs) + 4):
+            if s < len(runs):
+                for block in runs[s]:
+                    sort_pairs(block)
+            if 1 <= s <= len(runs):
+                for block in runs[s - 1]:
+                    transpose_and_copy_out(block)
+                for block in runs[s - 1]:
+                    quantise_x(block)
+            if windows_done < windows_quantised:
+                window_context(windows_done)
+                windows_done += 1
+            if tiles_finished < len(closed_tiles):
+                t = closed_tiles[tiles_finished]
+                finish_token_tile(t)
+                tiles_finished += 1
+                if tiles_finished % WINDOW_TILES == 0:
+                    quantise_window(windows_quantised)
+                    windows_quantised += 1
+            if 2 <= s <= len(runs) + 1:
+                for block in runs[s - 2]:
+                    project(block)
+                    if block[1] == CHUNKS - 1:
+                        closed_tiles.append(block[0])

@@ -87,19 +87,26 @@ def tile_localcontextprocessor_pa_k_kernel(
             )
             x_raw_of[(t, c)] = x_raw
 
-        w_planes = weights.tile([P, GROUPS, COLS], U8, align_bytes=64)
-        nc.vector.memset(w_planes[:].rearrange("p g n -> p (g n)").bitcast(I32), 0)
+        w_planes_of = {}
+        for c in range(CHUNKS):
+            w_planes = weights.tile([P, COLS], U8, name="w_planes_%d" % c, align_bytes=64)
+            nc.vector.memset(w_planes[:].bitcast(I32), 0)
+            w_planes_of[c] = w_planes
 
-        def load_weight_planes():
+        def load_weight_planes(c, quadrant):
+            first_row = quadrant * QUADRANT
             for scales, first_col in weight_scales:
-                rows = scales.bitcast(I32).rearrange("g (q r) n -> r q g n", r=PACK)
-                for r in range(PACK):
-                    nc.sync.dma_start(
-                        out=w_planes[
-                            r:P:QUADRANT, :, first_col : first_col + INNER
-                        ].bitcast(I32),
-                        in_=rows[r],
-                    )
+                nc.sync.dma_start(
+                    out=w_planes_of[c][
+                        first_row : first_row + CHUNK_GROUPS * PACK,
+                        first_col : first_col + INNER,
+                    ].bitcast(I32),
+                    in_=scales[
+                        c * CHUNK_GROUPS : (c + 1) * CHUNK_GROUPS,
+                        quadrant * PACK : (quadrant + 1) * PACK,
+                        :,
+                    ].bitcast(I32),
+                )
 
         w_words_of = {}
 
@@ -123,8 +130,7 @@ def tile_localcontextprocessor_pa_k_kernel(
         for c in range(CHUNKS):
             for t in range(WINDOW_TILES):
                 load_x(t, c)
-            if c == 0:
-                load_weight_planes()
+                load_weight_planes(c, t)
             for g in range(c * CHUNK_GROUPS, (c + 1) * CHUNK_GROUPS, LOAD_GROUPS):
                 load_weight_words(g)
         for t, c in blocks[CHUNKS * WINDOW_TILES :]:
@@ -186,7 +192,7 @@ def tile_localcontextprocessor_pa_k_kernel(
                     lhsT=x_words[:, tokens].bitcast(FP8X4),
                     lhsT_scale=x_plane[:, tokens],
                     rhs=w_words_of[group].bitcast(FP8X4),
-                    rhs_scale=w_planes[:, group, :],
+                    rhs_scale=w_planes_of[c][g * PACK : P, :],
                     start=(group == 0),
                     stop=(group == GROUPS - 1),
                 )

@@ -37,6 +37,7 @@ LOAD_GROUPS = 2
 RUN_BLOCKS = 2
 QUADRANT = 32
 HALF_HEADS = P // HEAD_DIM
+CONTEXT_LAG = 3
 
 FLOPS = 2 * TOKENS * FEATURES * COLS + 2 * WINDOWS * HEADS * WINDOW * HEAD_DIM * HEAD_DIM
 
@@ -263,9 +264,9 @@ def tile_localcontextprocessor_pa_k_kernel(
 
         closed_tiles = []
         tiles_finished = 0
-        windows_quantised = 0
+        quantised_at = []
         windows_done = 0
-        for s in range(len(runs) + 4):
+        for s in range(len(runs) + 3 + CONTEXT_LAG):
             if s < len(runs):
                 for block in runs[s]:
                     sort_pairs(block)
@@ -274,7 +275,7 @@ def tile_localcontextprocessor_pa_k_kernel(
                     transpose_and_copy_out(block)
                 for block in runs[s - 1]:
                     quantise_x(block)
-            if windows_done < windows_quantised:
+            if windows_done < len(quantised_at) and s >= quantised_at[windows_done] + CONTEXT_LAG:
                 window_context(windows_done)
                 windows_done += 1
             if tiles_finished < len(closed_tiles):
@@ -282,8 +283,8 @@ def tile_localcontextprocessor_pa_k_kernel(
                 finish_token_tile(t)
                 tiles_finished += 1
                 if tiles_finished % WINDOW_TILES == 0:
-                    quantise_window(windows_quantised)
-                    windows_quantised += 1
+                    quantise_window(len(quantised_at))
+                    quantised_at.append(s)
             if 2 <= s <= len(runs) + 1:
                 for block in runs[s - 2]:
                     project(block)

@@ -179,39 +179,39 @@ def tile_localcontextprocessor_pa_k_kernel(
             )
             x_codes_of[block] = (x_words, x_plane)
 
-        def project(block):
+        def project(block, first_col=0, width=COLS):
             t, c = block
             if c == 0:
-                acc = acc_psum.tile([P, COLS], F32)
-                acc_of[t] = acc
+                acc = acc_psum.tile([P, width], F32, tag="acc")
+                acc_of[(t, first_col)] = acc
             x_words, x_plane = x_codes_of[block]
+            cols = slice(first_col, first_col + width)
             for g in range(CHUNK_GROUPS):
                 group = c * CHUNK_GROUPS + g
                 tokens = slice(g * P, (g + 1) * P)
                 nc.tensor.matmul_mx(
-                    out=acc_of[t][:],
+                    out=acc_of[(t, first_col)][:],
                     lhsT=x_words[:, tokens].bitcast(FP8X4),
                     lhsT_scale=x_plane[:, tokens],
-                    rhs=w_words_of[group].bitcast(FP8X4),
-                    rhs_scale=w_planes_of[c][g * PACK : P, :],
+                    rhs=w_words_of[group][:, cols].bitcast(FP8X4),
+                    rhs_scale=w_planes_of[c][g * PACK : P, cols],
                     start=(group == 0),
                     stop=(group == GROUPS - 1),
                 )
 
         window_tiles_of = {}
 
-        def finish_token_tile(t):
+        def finish_k(t, k_sums):
             w, j = t // WINDOW_TILES, t % WINDOW_TILES
             if j == 0:
                 kf_grouped = window_pool.tile([P, INNER, PACK], BF16, align_bytes=64)
                 v_grouped = window_pool.tile([P, INNER, PACK], BF16, align_bytes=64)
                 window_tiles_of[w] = (kf_grouped, v_grouped)
-            kf_grouped, v_grouped = window_tiles_of[w]
-            acc = acc_of[t]
+            kf_grouped = window_tiles_of[w][0]
             exp_k = per_tile.tile([P, INNER], F32)
             relu_k = per_tile.tile([P, INNER], F32)
-            nc.scalar.activation(out=exp_k[:], in_=acc[:, 0:INNER], func=ACT.Exp)
-            nc.scalar.activation(out=relu_k[:], in_=acc[:, 0:INNER], func=ACT.Relu)
+            nc.scalar.activation(out=exp_k[:], in_=k_sums, func=ACT.Exp)
+            nc.scalar.activation(out=relu_k[:], in_=k_sums, func=ACT.Relu)
             nc.vector.scalar_tensor_tensor(
                 out=kf_grouped[:, :, j],
                 in0=exp_k[:],
@@ -220,30 +220,43 @@ def tile_localcontextprocessor_pa_k_kernel(
                 op0=ALU.min,
                 op1=ALU.add,
             )
-            nc.scalar.copy(out=v_grouped[:, :, j], in_=acc[:, INNER:COLS])
 
-        window_codes_of = {}
+        def finish_v(t, v_sums):
+            w, j = t // WINDOW_TILES, t % WINDOW_TILES
+            v_grouped = window_tiles_of[w][1]
+            nc.scalar.copy(out=v_grouped[:, :, j], in_=v_sums)
 
-        def quantise_window(w):
-            kf_grouped, v_grouped = window_tiles_of[w]
+        def finish_token_tile(t):
+            acc = acc_of[(t, 0)]
+            finish_k(t, acc[:, 0:INNER])
+            finish_v(t, acc[:, INNER:COLS])
+
+        kf_codes_of = {}
+        v_codes_of = {}
+
+        def quantise_kf(w):
             kf_words = window_pool.tile([P, INNER], U32, align_bytes=64)
             kf_plane = window_pool.tile([P, INNER], U8, align_bytes=64)
-            v_words = window_pool.tile([P, INNER], U32, align_bytes=64)
-            v_plane = window_pool.tile([P, INNER], U8, align_bytes=64)
             nc.vector.quantize_mx(
                 out=kf_words[:].bitcast(FP8X4),
                 scales=kf_plane[:],
-                in_=kf_grouped[:].rearrange("p n j -> p (n j)"),
+                in_=window_tiles_of[w][0][:].rearrange("p n j -> p (n j)"),
             )
+            kf_codes_of[w] = (kf_words, kf_plane)
+
+        def quantise_v(w):
+            v_words = window_pool.tile([P, INNER], U32, align_bytes=64)
+            v_plane = window_pool.tile([P, INNER], U8, align_bytes=64)
             nc.vector.quantize_mx(
                 out=v_words[:].bitcast(FP8X4),
                 scales=v_plane[:],
-                in_=v_grouped[:].rearrange("p n j -> p (n j)"),
+                in_=window_tiles_of[w][1][:].rearrange("p n j -> p (n j)"),
             )
-            window_codes_of[w] = (kf_words, kf_plane, v_words, v_plane)
+            v_codes_of[w] = (v_words, v_plane)
 
         def window_context(w):
-            kf_words, kf_plane, v_words, v_plane = window_codes_of[w]
+            kf_words, kf_plane = kf_codes_of[w]
+            v_words, v_plane = v_codes_of[w]
             products = acc_psum.tile([P, HEADS // HALF_HEADS, P], F32, tag="acc")
             for a in range(HEADS // HALF_HEADS):
                 cols = slice(a * P, (a + 1) * P)
@@ -266,7 +279,8 @@ def tile_localcontextprocessor_pa_k_kernel(
         tiles_finished = 0
         quantised_at = []
         windows_done = 0
-        for s in range(len(runs) + 3 + CONTEXT_LAG):
+        last_tile = TOKEN_TILES - 1
+        for s in range(len(runs) + 2):
             if s < len(runs):
                 for block in runs[s]:
                     sort_pairs(block)
@@ -283,10 +297,22 @@ def tile_localcontextprocessor_pa_k_kernel(
                 finish_token_tile(t)
                 tiles_finished += 1
                 if tiles_finished % WINDOW_TILES == 0:
-                    quantise_window(len(quantised_at))
+                    quantise_kf(len(quantised_at))
+                    quantise_v(len(quantised_at))
                     quantised_at.append(s)
             if 2 <= s <= len(runs) + 1:
                 for block in runs[s - 2]:
-                    project(block)
-                    if block[1] == CHUNKS - 1:
-                        closed_tiles.append(block[0])
+                    if block[0] == last_tile:
+                        project(block, 0, INNER)
+                    else:
+                        project(block)
+                        if block[1] == CHUNKS - 1:
+                            closed_tiles.append(block[0])
+
+        finish_k(last_tile, acc_of[(last_tile, 0)][:])
+        quantise_kf(WINDOWS - 1)
+        for c in range(CHUNKS):
+            project((last_tile, c), INNER, INNER)
+        finish_v(last_tile, acc_of[(last_tile, INNER)][:])
+        quantise_v(WINDOWS - 1)
+        window_context(WINDOWS - 1)

@@ -304,6 +304,8 @@ def tile_localcontextprocessor_pa_k_kernel(
                 for block in runs[s - 2]:
                     if block[0] == last_tile:
                         project(block, 0, INNER)
+                        if s - 2 < len(runs) - 1:
+                            project(block, INNER, INNER)
                     else:
                         project(block)
                         if block[1] == CHUNKS - 1:
@@ -311,8 +313,8 @@ def tile_localcontextprocessor_pa_k_kernel(
 
         finish_k(last_tile, acc_of[(last_tile, 0)][:])
         quantise_kf(WINDOWS - 1)
-        for c in range(CHUNKS):
-            project((last_tile, c), INNER, INNER)
+        for block in runs[-1]:
+            project(block, INNER, INNER)
         finish_v(last_tile, acc_of[(last_tile, INNER)][:])
         quantise_v(WINDOWS - 1)
         window_context(WINDOWS - 1)

@@ -33,7 +33,7 @@ CHUNKS = GROUPS // CHUNK_GROUPS
 BLOCK_FEATURES = CHUNK_GROUPS * K_PASS
 BLOCK_PAIRS = BLOCK_FEATURES // 2
 BANK_GROUPS = 2
-LOAD_GROUPS = 2
+LOAD_GROUPS = 4
 RUN_BLOCKS = 2
 QUADRANT = 32
 HALF_HEADS = P // HEAD_DIM

@@ -90,7 +90,7 @@ def tile_localcontextprocessor_pa_k_kernel(
 
         w_planes_of = {}
         for c in range(CHUNKS):
-            w_planes = weights.tile([P, COLS], U8, name="w_planes_%d" % c, align_bytes=64)
+            w_planes = weights.tile([P, COLS], U8, name="w_planes_%d" % c, align_bytes=256)
             nc.vector.memset(w_planes[:].bitcast(I32), 0)
             w_planes_of[c] = w_planes
 
@@ -113,7 +113,7 @@ def tile_localcontextprocessor_pa_k_kernel(
 
         def load_weight_words(first_group):
             w_words = weights.tile(
-                [P, LOAD_GROUPS, COLS], U32, name="w_words_%d" % first_group, align_bytes=64
+                [P, LOAD_GROUPS, COLS], U32, name="w_words_%d" % first_group, align_bytes=256
             )
             for words, first_col in weight_words:
                 rows = (
@@ -154,7 +154,7 @@ def tile_localcontextprocessor_pa_k_kernel(
 
         def transpose_and_copy_out(block):
             x_sorted = x_sorted_of[block]
-            grouped = stream.tile([P, BLOCK_FEATURES], BF16, align_bytes=64)
+            grouped = stream.tile([P, BLOCK_FEATURES], BF16, align_bytes=256)
             grouped_pairs = (
                 grouped[:].bitcast(F32).rearrange("p (g t u) -> p g t u", g=CHUNK_GROUPS, u=2)
             )
@@ -172,8 +172,8 @@ def tile_localcontextprocessor_pa_k_kernel(
             grouped_of[block] = grouped
 
         def quantise_x(block):
-            x_words = stream.tile([P, CHUNK_GROUPS * P], U32, align_bytes=64)
-            x_plane = stream.tile([P, CHUNK_GROUPS * P], U8, align_bytes=64)
+            x_words = stream.tile([P, CHUNK_GROUPS * P], U32, align_bytes=256)
+            x_plane = stream.tile([P, CHUNK_GROUPS * P], U8, align_bytes=256)
             nc.vector.quantize_mx(
                 out=x_words[:].bitcast(FP8X4), scales=x_plane[:], in_=grouped_of[block][:]
             )
@@ -204,8 +204,8 @@ def tile_localcontextprocessor_pa_k_kernel(
         def finish_k(t, k_sums):
             w, j = t // WINDOW_TILES, t % WINDOW_TILES
             if j == 0:
-                kf_grouped = window_pool.tile([P, INNER, PACK], BF16, align_bytes=64)
-                v_grouped = window_pool.tile([P, INNER, PACK], BF16, align_bytes=64)
+                kf_grouped = window_pool.tile([P, INNER, PACK], BF16, align_bytes=256)
+                v_grouped = window_pool.tile([P, INNER, PACK], BF16, align_bytes=256)
                 window_tiles_of[w] = (kf_grouped, v_grouped)
             kf_grouped = window_tiles_of[w][0]
             exp_k = per_tile.tile([P, INNER], F32)
@@ -235,8 +235,8 @@ def tile_localcontextprocessor_pa_k_kernel(
         v_codes_of = {}
 
         def quantise_kf(w):
-            kf_words = window_pool.tile([P, INNER], U32, align_bytes=64)
-            kf_plane = window_pool.tile([P, INNER], U8, align_bytes=64)
+            kf_words = window_pool.tile([P, INNER], U32, align_bytes=256)
+            kf_plane = window_pool.tile([P, INNER], U8, align_bytes=256)
             nc.vector.quantize_mx(
                 out=kf_words[:].bitcast(FP8X4),
                 scales=kf_plane[:],
@@ -245,8 +245,8 @@ def tile_localcontextprocessor_pa_k_kernel(
             kf_codes_of[w] = (kf_words, kf_plane)
 
         def quantise_v(w):
-            v_words = window_pool.tile([P, INNER], U32, align_bytes=64)
-            v_plane = window_pool.tile([P, INNER], U8, align_bytes=64)
+            v_words = window_pool.tile([P, INNER], U32, align_bytes=256)
+            v_plane = window_pool.tile([P, INNER], U8, align_bytes=256)
             nc.vector.quantize_mx(
                 out=v_words[:].bitcast(FP8X4),
                 scales=v_plane[:],

from contextlib import ExitStack

import concourse.mybir as mybir
from concourse.masks import make_identity

F32 = mybir.dt.float32
BF16 = mybir.dt.bfloat16
I32 = mybir.dt.int32
U32 = mybir.dt.uint32
U8 = mybir.dt.uint8
FP8X4 = mybir.dt.float8_e4m3fn_x4
ACT = mybir.ActivationFunctionType
ALU = mybir.AluOpType

P = 128
PACK = 4
K_PASS = P * PACK

TOKENS = 1024
FEATURES = 8192
WINDOW = 512
WINDOWS = TOKENS // WINDOW
HEADS = 8
HEAD_DIM = 32
INNER = HEADS * HEAD_DIM
COLS = 2 * INNER

GROUPS = FEATURES // K_PASS
WINDOW_TILES = WINDOW // P
TOKEN_TILES = TOKENS // P
CHUNK_GROUPS = 4
CHUNKS = GROUPS // CHUNK_GROUPS
BLOCK_FEATURES = CHUNK_GROUPS * K_PASS
BLOCK_PAIRS = BLOCK_FEATURES // 2
BANK_GROUPS = 2
LOAD_GROUPS = 4
RUN_BLOCKS = 2
QUADRANT = 32
HALF_HEADS = P // HEAD_DIM
CONTEXT_LAG = 3

FLOPS = 2 * TOKENS * FEATURES * COLS + 2 * WINDOWS * HEADS * WINDOW * HEAD_DIM * HEAD_DIM


def tile_localcontextprocessor_pa_k_kernel(
    tc, x, w_k_words, w_k_scales, w_v_words, w_v_scales, out
):
    nc = tc.nc

    blocks = [(t, c) for c in range(CHUNKS) for t in range(WINDOW_TILES)]
    blocks += [(t, c) for t in range(WINDOW_TILES, TOKEN_TILES) for c in range(CHUNKS)]
    runs = [blocks[i : i + RUN_BLOCKS] for i in range(0, len(blocks), RUN_BLOCKS)]

    x_tiles = x.flatten_outer_dims().rearrange("(w p j) d -> w j p d", p=P, j=PACK)
    out_rows = out.rearrange("w (a h) d e -> (h d) w a e", a=HEADS // HALF_HEADS)
    weight_words = [(w_k_words, 0), (w_v_words, INNER)]
    weight_scales = [(w_k_scales, 0), (w_v_scales, INNER)]

    with ExitStack() as stack:
        consts = stack.enter_context(tc.tile_pool(name="consts", bufs=1))
        weights = stack.enter_context(tc.tile_pool(name="weights", bufs=1))
        x_pool = stack.enter_context(tc.tile_pool(name="x_pool", bufs=len(blocks)))
        stream = stack.enter_context(tc.tile_pool(name="stream", bufs=2 * RUN_BLOCKS))
        per_tile = stack.enter_context(tc.tile_pool(name="per_tile", bufs=2))
        window_pool = stack.enter_context(tc.tile_pool(name="window_pool", bufs=1))
        flip_psum = stack.enter_context(tc.psum_pool(name="flip_psum", bufs=4))
        acc_psum = stack.enter_context(tc.psum_pool(name="acc_psum", bufs=4))
        stack.enter_context(tc.manual_schedule())

        warm = consts.tile([P, 1], F32)
        nc.vector.memset(warm[:], 0.0)
        nc.scalar.activation(out=warm[:], in_=warm[:], func=ACT.Exp)
        identity = consts.tile([P, P], F32)
        make_identity(nc, identity[:])

        x_raw_of = {}

        def load_x(t, c):
            x_raw = x_pool.tile([P, BLOCK_FEATURES], BF16)
            nc.sync.dma_start(
                out=x_raw[:],
                in_=x_tiles[
                    t // WINDOW_TILES,
                    t % WINDOW_TILES,
                    :,
                    c * BLOCK_FEATURES : (c + 1) * BLOCK_FEATURES,
                ],
            )
            x_raw_of[(t, c)] = x_raw

        w_planes_of = {}
        for c in range(CHUNKS):
            w_planes = weights.tile([P, COLS], U8, name="w_planes_%d" % c, align_bytes=256)
            nc.vector.memset(w_planes[:].bitcast(I32), 0)
            w_planes_of[c] = w_planes

        def load_weight_planes(c, quadrant):
            first_row = quadrant * QUADRANT
            for scales, first_col in weight_scales:
                nc.sync.dma_start(
                    out=w_planes_of[c][
                        first_row : first_row + CHUNK_GROUPS * PACK,
                        first_col : first_col + INNER,
                    ].bitcast(I32),
                    in_=scales[
                        c * CHUNK_GROUPS : (c + 1) * CHUNK_GROUPS,
                        quadrant * PACK : (quadrant + 1) * PACK,
                        :,
                    ].bitcast(I32),
                )

        w_words_of = {}

        def load_weight_words(first_group):
            w_words = weights.tile(
                [P, LOAD_GROUPS, COLS], U32, name="w_words_%d" % first_group, align_bytes=256
            )
            for words, first_col in weight_words:
                rows = (
                    words.rearrange("g p n t -> g p (n t)")
                    .bitcast(I32)
                    .rearrange("g p n -> p g n")
                )
                nc.sync.dma_start(
                    out=w_words[:, :, first_col : first_col + INNER].bitcast(I32),
                    in_=rows[:, first_group : first_group + LOAD_GROUPS, :],
                )
            for g in range(LOAD_GROUPS):
                w_words_of[first_group + g] = w_words[:, g, :]

        for c in range(CHUNKS):
            for t in range(WINDOW_TILES):
                load_x(t, c)
                load_weight_planes(c, t)
            for g in range(c * CHUNK_GROUPS, (c + 1) * CHUNK_GROUPS, LOAD_GROUPS):
                load_weight_words(g)
        for t, c in blocks[CHUNKS * WINDOW_TILES :]:
            load_x(t, c)

        x_sorted_of = {}
        grouped_of = {}
        x_codes_of = {}
        acc_of = {}

        def sort_pairs(block):
            x_sorted = stream.tile([P, CHUNK_GROUPS, 2, P], F32)
            nc.vector.tensor_copy(
                out=x_sorted[:],
                in_=x_raw_of[block][:]
                .bitcast(F32)
                .rearrange("p (g i u) -> p g u i", g=CHUNK_GROUPS, u=2),
            )
            x_sorted_of[block] = x_sorted

        def transpose_and_copy_out(block):
            x_sorted = x_sorted_of[block]
            grouped = stream.tile([P, BLOCK_FEATURES], BF16, align_bytes=256)
            grouped_pairs = (
                grouped[:].bitcast(F32).rearrange("p (g t u) -> p g t u", g=CHUNK_GROUPS, u=2)
            )
            for g0 in range(0, CHUNK_GROUPS, BANK_GROUPS):
                flipped = flip_psum.tile([P, BANK_GROUPS, 2, P], F32)
                for g in range(BANK_GROUPS):
                    for u in range(2):
                        nc.tensor.transpose(
                            flipped[:, g, u, :], x_sorted[:, g0 + g, u, :], identity[:]
                        )
                nc.scalar.copy(
                    out=grouped_pairs[:, g0 : g0 + BANK_GROUPS],
                    in_=flipped[:].rearrange("p g u t -> p g t u"),
                )
            grouped_of[block] = grouped

        def quantise_x(block):
            x_words = stream.tile([P, CHUNK_GROUPS * P], U32, align_bytes=256)
            x_plane = stream.tile([P, CHUNK_GROUPS * P], U8, align_bytes=256)
            nc.vector.quantize_mx(
                out=x_words[:].bitcast(FP8X4), scales=x_plane[:], in_=grouped_of[block][:]
            )
            x_codes_of[block] = (x_words, x_plane)

        def project(block, first_col=0, width=COLS):
            t, c = block
            if c == 0:
                acc = acc_psum.tile([P, width], F32, tag="acc")
                acc_of[(t, first_col)] = acc
            x_words, x_plane = x_codes_of[block]
            cols = slice(first_col, first_col + width)
            for g in range(CHUNK_GROUPS):
                group = c * CHUNK_GROUPS + g
                tokens = slice(g * P, (g + 1) * P)
                nc.tensor.matmul_mx(
                    out=acc_of[(t, first_col)][:],
                    lhsT=x_words[:, tokens].bitcast(FP8X4),
                    lhsT_scale=x_plane[:, tokens],
                    rhs=w_words_of[group][:, cols].bitcast(FP8X4),
                    rhs_scale=w_planes_of[c][g * PACK : P, cols],
                    start=(group == 0),
                    stop=(group == GROUPS - 1),
                )

        window_tiles_of = {}

        def finish_k(t, k_sums):
            w, j = t // WINDOW_TILES, t % WINDOW_TILES
            if j == 0:
                kf_grouped = window_pool.tile([P, INNER, PACK], BF16, align_bytes=256)
                v_grouped = window_pool.tile([P, INNER, PACK], BF16, align_bytes=256)
                window_tiles_of[w] = (kf_grouped, v_grouped)
            kf_grouped = window_tiles_of[w][0]
            exp_k = per_tile.tile([P, INNER], F32)
            relu_k = per_tile.tile([P, INNER], F32)
            nc.scalar.activation(out=exp_k[:], in_=k_sums, func=ACT.Exp)
            nc.scalar.activation(out=relu_k[:], in_=k_sums, func=ACT.Relu)
            nc.vector.scalar_tensor_tensor(
                out=kf_grouped[:, :, j],
                in0=exp_k[:],
                scalar=1.0,
                in1=relu_k[:],
                op0=ALU.min,
                op1=ALU.add,
            )

        def finish_v(t, v_sums):
            w, j = t // WINDOW_TILES, t % WINDOW_TILES
            v_grouped = window_tiles_of[w][1]
            nc.scalar.copy(out=v_grouped[:, :, j], in_=v_sums)

        def finish_token_tile(t):
            acc = acc_of[(t, 0)]
            finish_k(t, acc[:, 0:INNER])
            finish_v(t, acc[:, INNER:COLS])

        kf_codes_of = {}
        v_codes_of = {}

        def quantise_kf(w):
            kf_words = window_pool.tile([P, INNER], U32, align_bytes=256)
            kf_plane = window_pool.tile([P, INNER], U8, align_bytes=256)
            nc.vector.quantize_mx(
                out=kf_words[:].bitcast(FP8X4),
                scales=kf_plane[:],
                in_=window_tiles_of[w][0][:].rearrange("p n j -> p (n j)"),
            )
            kf_codes_of[w] = (kf_words, kf_plane)

        def quantise_v(w):
            v_words = window_pool.tile([P, INNER], U32, align_bytes=256)
            v_plane = window_pool.tile([P, INNER], U8, align_bytes=256)
            nc.vector.quantize_mx(
                out=v_words[:].bitcast(FP8X4),
                scales=v_plane[:],
                in_=window_tiles_of[w][1][:].rearrange("p n j -> p (n j)"),
            )
            v_codes_of[w] = (v_words, v_plane)

        def window_context(w):
            kf_words, kf_plane = kf_codes_of[w]
            v_words, v_plane = v_codes_of[w]
            products = acc_psum.tile([P, HEADS // HALF_HEADS, P], F32, tag="acc")
            for a in range(HEADS // HALF_HEADS):
                cols = slice(a * P, (a + 1) * P)
                nc.tensor.matmul_mx(
                    out=products[:, a, :],
                    lhsT=kf_words[:, cols].bitcast(FP8X4),
                    lhsT_scale=kf_plane[:, cols],
                    rhs=v_words[:, cols].bitcast(FP8X4),
                    rhs_scale=v_plane[:, cols],
                    start=True,
                    stop=True,
                )
            context = window_pool.tile([P, HEADS // HALF_HEADS, HEAD_DIM], F32)
            for h in range(HALF_HEADS):
                rows = slice(h * HEAD_DIM, (h + 1) * HEAD_DIM)
                nc.vector.tensor_copy(out=context[rows], in_=products[rows, :, rows])
            nc.sync.dma_start(out=out_rows[:, w], in_=context[:])

        closed_tiles = []
        tiles_finished = 0
        quantised_at = []
        windows_done = 0
        last_tile = TOKEN_TILES - 1
        for s in range(len(runs) + 2):
            if s < len(runs):
                for block in runs[s]:
                    sort_pairs(block)
            if 1 <= s <= len(runs):
                for block in runs[s - 1]:
                    transpose_and_copy_out(block)
                for block in runs[s - 1]:
                    quantise_x(block)
            if windows_done < len(quantised_at) and s >= quantised_at[windows_done] + CONTEXT_LAG:
                window_context(windows_done)
                windows_done += 1
            if tiles_finished < len(closed_tiles):
                t = closed_tiles[tiles_finished]
                finish_token_tile(t)
                tiles_finished += 1
                if tiles_finished % WINDOW_TILES == 0:
                    quantise_kf(len(quantised_at))
                    quantise_v(len(quantised_at))
                    quantised_at.append(s)
            if 2 <= s <= len(runs) + 1:
                for block in runs[s - 2]:
                    if block[0] == last_tile:
                        project(block, 0, INNER)
                        if s - 2 < len(runs) - 1:
                            project(block, INNER, INNER)
                    else:
                        project(block)
                        if block[1] == CHUNKS - 1:
                            closed_tiles.append(block[0])

        finish_k(last_tile, acc_of[(last_tile, 0)][:])
        quantise_kf(WINDOWS - 1)
        for block in runs[-1]:
            project(block, INNER, INNER)
        finish_v(last_tile, acc_of[(last_tile, INNER)][:])
        quantise_v(WINDOWS - 1)
        window_context(WINDOWS - 1)
